import numpy as np
import ml_dtypes


def mxq(x, axis, fmt="e4m3"):
    dtype, down = {"e4m3": (ml_dtypes.float8_e4m3fn, 7), "e5m2": (ml_dtypes.float8_e5m2, 14)}[fmt]
    v = np.moveaxis(np.asarray(x, np.float32).astype(ml_dtypes.bfloat16).astype(np.float64), axis, -1)
    blocks = v.reshape(v.shape[:-1] + (-1, 32))
    amax = np.abs(blocks).max(-1, keepdims=True)
    byte = np.maximum(np.where(amax > 0, np.frexp(amax)[1] - 1 + 127, 0) - down, 1)
    scale = np.exp2(byte - 127.0)
    codes = (blocks / scale).astype(np.float32).astype(dtype).astype(np.float64)
    return np.moveaxis((codes * scale).reshape(v.shape), -1, axis)


WIDE = False


def mx_kscale(k):
    if not WIDE:
        return np.ones(k)
    levels = np.array([20, -20, 10, -10, 0])
    a = np.random.permutation(np.resize(levels, k // 512 * 4)).reshape(k // 512, 4)
    idx = np.arange(k)
    return np.exp2(a[idx // 512, idx % 128 // 32])


BF16 = ml_dtypes.bfloat16


def bf(x):
    return np.asarray(x, np.float32).astype(BF16)


def f64(x):
    return np.asarray(x).astype(np.float64)


P = 16
B, C, IH, IW = 16, 4, 256, 256
D = 1024
DIN = C * P * P
GH, GW = IH // P, IW // P
NP = GH * GW
SEQ = NP + 1
T = B * NP


def _patchify(x):
    nb, nc_, h, w = x.shape
    gh, gw = h // P, w // P
    x = x.reshape(nb, nc_, gh, P, gw, P)
    x = x.transpose(0, 2, 4, 1, 3, 5)
    return x.reshape(nb, gh * gw, nc_ * P * P)


def setup_inputs():
    s = mx_kscale(T)
    sx = np.repeat(np.repeat(s.reshape(B, GH, GW), P, axis=1), P, axis=2)[:, None]
    sg = np.ones((B, SEQ, 1))
    sg[:, 1:, 0] = s.reshape(B, NP)
    x = np.random.standard_normal((B, C, IH, IW)) * sx
    W = np.random.standard_normal((D, DIN)) * 0.03
    b = np.random.standard_normal(D) * 0.1
    class_token = np.random.standard_normal(D)
    pos_emb = np.random.standard_normal((SEQ, D))
    g = np.random.standard_normal((B, SEQ, D)) * np.exp2(np.random.randint(-12, 1, (B, SEQ, 1))) * 0.25 / sg
    return {"x": bf(x), "W": bf(W), "b": bf(b), "class_token": bf(class_token),
            "pos_emb": bf(pos_emb), "grad_out": bf(g)}


def reference(x, W, b, class_token, pos_emb, grad_out):
    patches = _patchify(f64(x)).reshape(-1, DIN)
    g = f64(grad_out)[:, 1:, :].reshape(-1, D)
    return mxq(g, 0, "e5m2").T @ mxq(patches, 0, "e4m3")

@@ -1,0 +1,205 @@
+from contextlib import ExitStack
+
+import concourse.mybir as mybir
+
+BF16 = mybir.dt.bfloat16
+F32 = mybir.dt.float32
+U32 = mybir.dt.uint32
+U8 = mybir.dt.uint8
+E4 = mybir.dt.float8_e4m3fn_x4
+E5 = mybir.dt.float8_e5m2_x4
+
+FLOPS = 2 * 4096 * 1024 * 1024
+BYTES = 16 * 4 * 256 * 256 * 2 + 16 * 256 * 1024 * 2 + 1024 * 1024 * 4
+
+PLAN = "W"
+SKEW = True
+RAW_BUFS = 8
+
+
+def parts(a_x, r):
+    if PLAN == "W":
+        return [(64 * a_x + r, 0, 16)]
+    if a_x == 0:
+        return [(32 + r, 0, 16)]
+    return [(r, 0, 8), (96 + r, 8, 8)]
+
+
+def tile_patchpositionembedding_kernel(tc, x, W, b, class_token, pos_emb, grad_out, out):
+    nc = tc.nc
+    units = []
+    for a_y in range(2):
+        units += [("x", a_y, 0), ("x", a_y, 1)]
+        units += [("g", a_y, gq) for gq in range(4)]
+    units += [("x", 0, 2), ("x", 0, 3), ("x", 1, 2), ("x", 1, 3)]
+    groups = [("xc", 0, 0, [0]), ("xc", 0, 1, [1])]
+    groups += [("g", 0, gq, [2 + gq]) for gq in range(4)]
+    groups += [("xp", 1, 0, 0, [6, 7]), ("xp", 1, 0, 1, [6, 7])]
+    groups += [("g", 1, gq, [8 + gq]) for gq in range(4)]
+    groups += [("xp", 0, 1, 0, [12, 13]), ("xp", 0, 1, 1, [12, 13])]
+    groups += [("xp", 1, 1, 0, [14, 15]), ("xp", 1, 1, 1, [14, 15])]
+    last_reader = {}
+    for i, grp in enumerate(groups):
+        for u in grp[-1]:
+            last_reader[u] = i
+
+    with ExitStack() as ctx:
+        keep = ctx.enter_context(tc.tile_pool(name="keep", bufs=1))
+        rawp = ctx.enter_context(tc.tile_pool(name="rawp", bufs=RAW_BUFS))
+        grpp = ctx.enter_context(tc.tile_pool(name="grpp", bufs=3))
+        outp = ctx.enter_context(tc.tile_pool(name="outp", bufs=8))
+        psum = ctx.enter_context(tc.psum_pool(name="psum", bufs=1))
+        ctx.enter_context(tc.manual_schedule())
+
+        xc = keep.tile([128, 8192], U32, name="xc", align_bytes=64)
+        xs = keep.tile([128, 8192], U8, name="xs", align_bytes=64)
+        gc = keep.tile([128, 8192], U32, name="gc", align_bytes=64)
+        gs = keep.tile([128, 8192], U8, name="gs", align_bytes=64)
+
+        raw = {}
+
+        def load_piece(u, a_x, r, p0, b0, nb):
+            kind, a_y, sel = units[u]
+            gh = 8 * (r // 2) + 4 * a_x + 2 * a_y + (r % 2)
+            dst = raw[u][p0 : p0 + 4 * nb - 3 : 4, :]
+            if kind == "x":
+                src = x[b0 : b0 + nb, sel : sel + 1, gh * 16 : gh * 16 + 16, :].rearrange("b c h w -> b (c h w)")
+            else:
+                t0 = 1 + gh * 16 + sel * 4
+                src = grad_out[b0 : b0 + nb, t0 : t0 + 4, :].rearrange("b t e -> b (t e)")
+            nc.sync.dma_start(out=dst, in_=src)
+
+        def load_unit(u):
+            if u not in raw:
+                raw[u] = rawp.tile([128, 4096], BF16, name="raw", tag="raw", align_bytes=64)
+            for r in range(4):
+                for a_x in range(2):
+                    if SKEW and u == 15 and r == 0 and a_x == 1:
+                        load_piece(u, 1, 0, 96, 8, 8)
+                        continue
+                    for p0, b0, nb in parts(a_x, r):
+                        load_piece(u, a_x, r, p0, b0, nb)
+
+        def x_base(a_y, h, gq):
+            return ((a_y * 2 + h) * 4 + gq) * 512
+
+        grouped = {}
+
+        def x_granule(eng_copy, i, slot, u, gq):
+            src = raw[u][:].rearrange("p (ph gq j pw) -> p gq ph pw j", ph=16, gq=4, j=4, pw=16)[:, gq]
+            dst = grouped[i][:, slot * 1024 : slot * 1024 + 1024].rearrange(
+                "p (ph pw j) -> p ph pw j", ph=16, pw=16, j=4
+            )
+            eng_copy(out=dst, in_=src)
+
+        def copies(i):
+            grp = groups[i]
+            grouped[i] = grpp.tile([128, 4096], BF16, name="grouped", tag="grouped", align_bytes=64)
+            if grp[0] == "g":
+                src = raw[grp[3][0]][:].rearrange("p (j e) -> p e j", j=4)
+                dst = grouped[i][:].rearrange("p (e j) -> p e j", j=4)
+                nc.vector.tensor_copy(out=dst[:, 0:512, :], in_=src[:, 0:512, :])
+                nc.scalar.copy(out=dst[:, 512:1024, :], in_=src[:, 512:1024, :])
+            elif grp[0] == "xc":
+                u = grp[3][0]
+                x_granule(nc.vector.tensor_copy, i, 0, u, 0)
+                x_granule(nc.vector.tensor_copy, i, 1, u, 1)
+                x_granule(nc.scalar.copy, i, 2, u, 2)
+                x_granule(nc.scalar.copy, i, 3, u, 3)
+            else:
+                pair = grp[3]
+                u0, u1 = grp[4]
+                x_granule(nc.vector.tensor_copy, i, 0, u0, 2 * pair)
+                x_granule(nc.vector.tensor_copy, i, 1, u1, 2 * pair)
+                x_granule(nc.scalar.copy, i, 2, u0, 2 * pair + 1)
+                x_granule(nc.scalar.copy, i, 3, u1, 2 * pair + 1)
+
+        def quantise(i):
+            grp = groups[i]
+            t = grouped[i]
+            if grp[0] == "g":
+                o = (grp[1] * 4 + grp[2]) * 1024
+                nc.vector.quantize_mx(out=gc[:, o : o + 1024].bitcast(E5), scales=gs[:, o : o + 1024], in_=t[:])
+            elif grp[0] == "xc":
+                a_y, c = grp[1], grp[2]
+                for gq in range(4):
+                    o = x_base(a_y, c // 2, gq) + (c % 2) * 256
+                    nc.vector.quantize_mx(
+                        out=xc[:, o : o + 256].bitcast(E4),
+                        scales=xs[:, o : o + 256],
+                        in_=t[:, gq * 1024 : gq * 1024 + 1024],
+                    )
+            else:
+                o = x_base(grp[1], grp[2], 2 * grp[3])
+                nc.vector.quantize_mx(out=xc[:, o : o + 1024].bitcast(E4), scales=xs[:, o : o + 1024], in_=t[:])
+
+        acc = {}
+
+        def new_banks():
+            for m in range(8):
+                acc[m] = psum.tile([128, 512], F32, name="acc%d" % m)
+
+        def mm(m, h, a_y, gq):
+            k = a_y * 4 + gq
+            go = k * 1024 + m * 128
+            xo = x_base(a_y, h, gq)
+            nc.tensor.matmul_mx(
+                out=acc[m][:],
+                lhsT=gc[:, go : go + 128].bitcast(E5),
+                lhsT_scale=gs[:, go : go + 128],
+                rhs=xc[:, xo : xo + 512].bitcast(E4),
+                rhs_scale=xs[:, xo : xo + 512],
+                start=(k == 0),
+                stop=(k == 7),
+            )
+
+        def multiply(i):
+            grp = groups[i]
+            if grp[0] == "g":
+                for m in range(8):
+                    mm(m, 0, grp[1], grp[2])
+            elif grp[0] == "xp" and grp[2] == 1:
+                for m in range(8):
+                    mm(m, 1, grp[1], 2 * grp[3])
+                    mm(m, 1, grp[1], 2 * grp[3] + 1)
+
+        res = {}
+
+        def evacuate(eng_copy, m):
+            res[m] = outp.tile([128, 512], F32, name="res", tag="res")
+            eng_copy(out=res[m][:], in_=acc[m][:])
+
+        def store(m, h):
+            nc.sync.dma_start(out=out[m * 128 : m * 128 + 128, h * 512 : h * 512 + 512], in_=res[m][:])
+
+        if SKEW:
+            raw[15] = keep.tile([128, 4096], BF16, name="raw15", align_bytes=64)
+            load_piece(15, 1, 0, 64, 0, 8)
+        n_rot = 15 if SKEW else 16
+        next_unit = 0
+        while next_unit < RAW_BUFS:
+            load_unit(next_unit)
+            next_unit += 1
+        new_banks()
+        for i in range(len(groups) + 1):
+            if i == 13:
+                for m in (0, 2, 4, 6):
+                    evacuate(nc.scalar.copy, m)
+            if i < len(groups):
+                copies(i)
+                while next_unit < 16 and (next_unit >= n_rot or last_reader[next_unit - RAW_BUFS] <= i):
+                    load_unit(next_unit)
+                    next_unit += 1
+            if i >= 1:
+                quantise(i - 1)
+            if i == 13:
+                for m in (1, 3, 5, 7):
+                    evacuate(nc.vector.tensor_copy, m)
+                for m in range(8):
+                    store(m, 0)
+                new_banks()
+            if i >= 1:
+                multiply(i - 1)
+        for m in range(8):
+            evacuate(nc.scalar.copy if m % 2 == 0 else nc.vector.tensor_copy, m)
+            store(m, 1)

@@ -12,8 +12,8 @@ E5 = mybir.dt.float8_e5m2_x4
 FLOPS = 2 * 4096 * 1024 * 1024
 BYTES = 16 * 4 * 256 * 256 * 2 + 16 * 256 * 1024 * 2 + 1024 * 1024 * 4
 
-PLAN = "W"
-SKEW = True
+PLAN = "B"
+SKEW = False
 RAW_BUFS = 8
 
 

@@ -12,40 +12,21 @@ E5 = mybir.dt.float8_e5m2_x4
 FLOPS = 2 * 4096 * 1024 * 1024
 BYTES = 16 * 4 * 256 * 256 * 2 + 16 * 256 * 1024 * 2 + 1024 * 1024 * 4
 
-PLAN = "B"
-SKEW = False
-RAW_BUFS = 8
-
-
-def parts(a_x, r):
-    if PLAN == "W":
-        return [(64 * a_x + r, 0, 16)]
-    if a_x == 0:
-        return [(32 + r, 0, 16)]
-    return [(r, 0, 8), (96 + r, 8, 8)]
+G3DIM = False
+WINDOWS = ((32, 0, 16, 1), (0, 8, 8, 0), (96, 0, 8, 0))
 
 
 def tile_patchpositionembedding_kernel(tc, x, W, b, class_token, pos_emb, grad_out, out):
     nc = tc.nc
-    units = []
+    groups = []
     for a_y in range(2):
-        units += [("x", a_y, 0), ("x", a_y, 1)]
-        units += [("g", a_y, gq) for gq in range(4)]
-    units += [("x", 0, 2), ("x", 0, 3), ("x", 1, 2), ("x", 1, 3)]
-    groups = [("xc", 0, 0, [0]), ("xc", 0, 1, [1])]
-    groups += [("g", 0, gq, [2 + gq]) for gq in range(4)]
-    groups += [("xp", 1, 0, 0, [6, 7]), ("xp", 1, 0, 1, [6, 7])]
-    groups += [("g", 1, gq, [8 + gq]) for gq in range(4)]
-    groups += [("xp", 0, 1, 0, [12, 13]), ("xp", 0, 1, 1, [12, 13])]
-    groups += [("xp", 1, 1, 0, [14, 15]), ("xp", 1, 1, 1, [14, 15])]
-    last_reader = {}
-    for i, grp in enumerate(groups):
-        for u in grp[-1]:
-            last_reader[u] = i
+        groups += [("x", a_y, 0, 0), ("x", a_y, 0, 1)]
+        groups += [("g", a_y, gq) for gq in range(4)]
+    groups += [("x", 0, 1, 0), ("x", 0, 1, 1)]
 
     with ExitStack() as ctx:
         keep = ctx.enter_context(tc.tile_pool(name="keep", bufs=1))
-        rawp = ctx.enter_context(tc.tile_pool(name="rawp", bufs=RAW_BUFS))
+        rawp = ctx.enter_context(tc.tile_pool(name="rawp", bufs=3))
         grpp = ctx.enter_context(tc.tile_pool(name="grpp", bufs=3))
         outp = ctx.enter_context(tc.tile_pool(name="outp", bufs=8))
         psum = ctx.enter_context(tc.psum_pool(name="psum", bufs=1))
@@ -56,82 +37,94 @@ def tile_patchpositionembedding_kernel(tc, x, W, b, class_token, pos_emb, grad_o
         gc = keep.tile([128, 8192], U32, name="gc", align_bytes=64)
         gs = keep.tile([128, 8192], U8, name="gs", align_bytes=64)
 
-        raw = {}
+        xtile = {}
+        gtile = {}
 
-        def load_piece(u, a_x, r, p0, b0, nb):
-            kind, a_y, sel = units[u]
-            gh = 8 * (r // 2) + 4 * a_x + 2 * a_y + (r % 2)
-            dst = raw[u][p0 : p0 + 4 * nb - 3 : 4, :]
-            if kind == "x":
-                src = x[b0 : b0 + nb, sel : sel + 1, gh * 16 : gh * 16 + 16, :].rearrange("b c h w -> b (c h w)")
-            else:
-                t0 = 1 + gh * 16 + sel * 4
-                src = grad_out[b0 : b0 + nb, t0 : t0 + 4, :].rearrange("b t e -> b (t e)")
-            nc.sync.dma_start(out=dst, in_=src)
-
-        def load_unit(u):
-            if u not in raw:
-                raw[u] = rawp.tile([128, 4096], BF16, name="raw", tag="raw", align_bytes=64)
+        def load_x(a_y, h):
+            t = rawp.tile([128, 8192], BF16, name="xraw", tag="xraw", align_bytes=64)
+            xtile[(a_y, h)] = t
             for r in range(4):
-                for a_x in range(2):
-                    if SKEW and u == 15 and r == 0 and a_x == 1:
-                        load_piece(u, 1, 0, 96, 8, 8)
-                        continue
-                    for p0, b0, nb in parts(a_x, r):
-                        load_piece(u, a_x, r, p0, b0, nb)
+                for base, b0, nb, a_x in WINDOWS:
+                    gh = 8 * (r // 2) + 4 * a_x + 2 * a_y + (r % 2)
+                    p0 = base + r
+                    nc.sync.dma_start(
+                        out=t[p0 : p0 + 4 * nb - 3 : 4, :].rearrange("p (c f) -> p c f", c=2),
+                        in_=x[b0 : b0 + nb, 2 * h : 2 * h + 2, gh * 16 : gh * 16 + 16, :].rearrange(
+                            "b c h w -> b c (h w)"
+                        ),
+                    )
+
+        def load_g(a_y, pr):
+            t = rawp.tile([128, 8192], BF16, name="graw", tag="graw", align_bytes=64)
+            gtile[(a_y, pr)] = t
+            if G3DIM:
+                for gh0 in range(2):
+                    for base, b0, nb, a_x in WINDOWS:
+                        p0 = base + gh0
+                        off = ((4 * a_x + 2 * a_y + gh0) * 16 + pr * 8) * 1024
+                        nc.sync.dma_start(
+                            out=t[p0 : p0 + 4 * nb - 1 : 2, :].rearrange("(b g) f -> b g f", g=2),
+                            in_=grad_out[b0 : b0 + nb, 1:257, :].rearrange("b (g t) e -> b g (t e)", g=2)[
+                                :, :, off : off + 8192
+                            ],
+                        )
+            else:
+                for r in range(4):
+                    for base, b0, nb, a_x in WINDOWS:
+                        gh = 8 * (r // 2) + 4 * a_x + 2 * a_y + (r % 2)
+                        t0 = 1 + gh * 16 + pr * 8
+                        p0 = base + r
+                        nc.sync.dma_start(
+                            out=t[p0 : p0 + 4 * nb - 3 : 4, :],
+                            in_=grad_out[b0 : b0 + nb, t0 : t0 + 8, :].rearrange("b t e -> b (t e)"),
+                        )
 
         def x_base(a_y, h, gq):
             return ((a_y * 2 + h) * 4 + gq) * 512
 
-        grouped = {}
-
-        def x_granule(eng_copy, i, slot, u, gq):
-            src = raw[u][:].rearrange("p (ph gq j pw) -> p gq ph pw j", ph=16, gq=4, j=4, pw=16)[:, gq]
-            dst = grouped[i][:, slot * 1024 : slot * 1024 + 1024].rearrange(
-                "p (ph pw j) -> p ph pw j", ph=16, pw=16, j=4
+        def x_copy(eng_copy, dst_tile, slot, a_y, h, gq):
+            src = xtile[(a_y, h)][:].rearrange("p (cph gq j pw) -> p gq cph pw j", cph=32, gq=4, j=4, pw=16)[:, gq]
+            dst = dst_tile[:, slot * 2048 : slot * 2048 + 2048].rearrange(
+                "p (cph pw j) -> p cph pw j", cph=32, pw=16, j=4
             )
             eng_copy(out=dst, in_=src)
 
+        def x_quant(src_tile, slot, n, a_y, h, gq):
+            o = x_base(a_y, h, gq)
+            nc.vector.quantize_mx(
+                out=xc[:, o : o + 512 * n].bitcast(E4),
+                scales=xs[:, o : o + 512 * n],
+                in_=src_tile[:, slot * 2048 : (slot + n) * 2048],
+            )
+
+        grouped = {}
+
+        def new_grouped(i):
+            grouped[i] = grpp.tile([128, 4096], BF16, name="grouped", tag="grouped", align_bytes=64)
+            return grouped[i]
+
         def copies(i):
             grp = groups[i]
-            grouped[i] = grpp.tile([128, 4096], BF16, name="grouped", tag="grouped", align_bytes=64)
+            t = new_grouped(i)
             if grp[0] == "g":
-                src = raw[grp[3][0]][:].rearrange("p (j e) -> p e j", j=4)
-                dst = grouped[i][:].rearrange("p (e j) -> p e j", j=4)
+                o = (grp[2] % 2) * 4096
+                src = gtile[(grp[1], grp[2] // 2)][:, o : o + 4096].rearrange("p (j e) -> p e j", j=4)
+                dst = t[:].rearrange("p (e j) -> p e j", j=4)
                 nc.vector.tensor_copy(out=dst[:, 0:512, :], in_=src[:, 0:512, :])
                 nc.scalar.copy(out=dst[:, 512:1024, :], in_=src[:, 512:1024, :])
-            elif grp[0] == "xc":
-                u = grp[3][0]
-                x_granule(nc.vector.tensor_copy, i, 0, u, 0)
-                x_granule(nc.vector.tensor_copy, i, 1, u, 1)
-                x_granule(nc.scalar.copy, i, 2, u, 2)
-                x_granule(nc.scalar.copy, i, 3, u, 3)
             else:
-                pair = grp[3]
-                u0, u1 = grp[4]
-                x_granule(nc.vector.tensor_copy, i, 0, u0, 2 * pair)
-                x_granule(nc.vector.tensor_copy, i, 1, u1, 2 * pair)
-                x_granule(nc.scalar.copy, i, 2, u0, 2 * pair + 1)
-                x_granule(nc.scalar.copy, i, 3, u1, 2 * pair + 1)
+                x_copy(nc.vector.tensor_copy, t, 0, grp[1], grp[2], 2 * grp[3])
+                x_copy(nc.scalar.copy, t, 1, grp[1], grp[2], 2 * grp[3] + 1)
 
         def quantise(i):
             grp = groups[i]
-            t = grouped[i]
             if grp[0] == "g":
                 o = (grp[1] * 4 + grp[2]) * 1024
-                nc.vector.quantize_mx(out=gc[:, o : o + 1024].bitcast(E5), scales=gs[:, o : o + 1024], in_=t[:])
-            elif grp[0] == "xc":
-                a_y, c = grp[1], grp[2]
-                for gq in range(4):
-                    o = x_base(a_y, c // 2, gq) + (c % 2) * 256
-                    nc.vector.quantize_mx(
-                        out=xc[:, o : o + 256].bitcast(E4),
-                        scales=xs[:, o : o + 256],
-                        in_=t[:, gq * 1024 : gq * 1024 + 1024],
-                    )
+                nc.vector.quantize_mx(
+                    out=gc[:, o : o + 1024].bitcast(E5), scales=gs[:, o : o + 1024], in_=grouped[i][:]
+                )
             else:
-                o = x_base(grp[1], grp[2], 2 * grp[3])
-                nc.vector.quantize_mx(out=xc[:, o : o + 1024].bitcast(E4), scales=xs[:, o : o + 1024], in_=t[:])
+                x_quant(grouped[i], 0, 2, grp[1], grp[2], 2 * grp[3])
 
         acc = {}
 
@@ -158,7 +151,7 @@ def tile_patchpositionembedding_kernel(tc, x, W, b, class_token, pos_emb, grad_o
             if grp[0] == "g":
                 for m in range(8):
                     mm(m, 0, grp[1], grp[2])
-            elif grp[0] == "xp" and grp[2] == 1:
+            elif grp[2] == 1:
                 for m in range(8):
                     mm(m, 1, grp[1], 2 * grp[3])
                     mm(m, 1, grp[1], 2 * grp[3] + 1)
@@ -172,24 +165,23 @@ def tile_patchpositionembedding_kernel(tc, x, W, b, class_token, pos_emb, grad_o
         def store(m, h):
             nc.sync.dma_start(out=out[m * 128 : m * 128 + 128, h * 512 : h * 512 + 512], in_=res[m][:])
 
-        if SKEW:
-            raw[15] = keep.tile([128, 4096], BF16, name="raw15", align_bytes=64)
-            load_piece(15, 1, 0, 64, 0, 8)
-        n_rot = 15 if SKEW else 16
-        next_unit = 0
-        while next_unit < RAW_BUFS:
-            load_unit(next_unit)
-            next_unit += 1
+        load_x(0, 0)
+        load_g(0, 0)
+        load_g(0, 1)
+        load_x(1, 0)
+        load_g(1, 0)
         new_banks()
-        for i in range(len(groups) + 1):
+        n = len(groups)
+        for i in range(n + 1):
             if i == 13:
                 for m in (0, 2, 4, 6):
                     evacuate(nc.scalar.copy, m)
-            if i < len(groups):
+            if i < n:
                 copies(i)
-                while next_unit < 16 and (next_unit >= n_rot or last_reader[next_unit - RAW_BUFS] <= i):
-                    load_unit(next_unit)
-                    next_unit += 1
+            if i == 3:
+                load_g(1, 1)
+                load_x(0, 1)
+                load_x(1, 1)
             if i >= 1:
                 quantise(i - 1)
             if i == 13:
@@ -200,6 +192,22 @@ def tile_patchpositionembedding_kernel(tc, x, W, b, class_token, pos_emb, grad_o
                 new_banks()
             if i >= 1:
                 multiply(i - 1)
+        ta = new_grouped(14)
+        tb = new_grouped(15)
+        x_copy(nc.vector.tensor_copy, ta, 0, 1, 1, 0)
+        x_copy(nc.scalar.copy, ta, 1, 1, 1, 1)
+        x_quant(ta, 0, 1, 1, 1, 0)
         for m in range(8):
+            mm(m, 1, 1, 0)
+        x_copy(nc.vector.tensor_copy, tb, 0, 1, 1, 2)
+        x_copy(nc.scalar.copy, tb, 1, 1, 1, 3)
+        x_quant(ta, 1, 1, 1, 1, 1)
+        for m in range(8):
+            mm(m, 1, 1, 1)
+        x_quant(tb, 0, 1, 1, 1, 2)
+        x_quant(tb, 1, 1, 1, 1, 3)
+        for m in range(8):
+            mm(m, 1, 1, 2)
+            mm(m, 1, 1, 3)
             evacuate(nc.scalar.copy if m % 2 == 0 else nc.vector.tensor_copy, m)
             store(m, 1)

@@ -12,21 +12,40 @@ E5 = mybir.dt.float8_e5m2_x4
 FLOPS = 2 * 4096 * 1024 * 1024
 BYTES = 16 * 4 * 256 * 256 * 2 + 16 * 256 * 1024 * 2 + 1024 * 1024 * 4
 
-G3DIM = False
-WINDOWS = ((32, 0, 16, 1), (0, 8, 8, 0), (96, 0, 8, 0))
+PLAN = "B"
+SKEW = False
+RAW_BUFS = 8
+
+
+def parts(a_x, r):
+    if PLAN == "W":
+        return [(64 * a_x + r, 0, 16)]
+    if a_x == 0:
+        return [(32 + r, 0, 16)]
+    return [(r, 0, 8), (96 + r, 8, 8)]
 
 
 def tile_patchpositionembedding_kernel(tc, x, W, b, class_token, pos_emb, grad_out, out):
     nc = tc.nc
-    groups = []
+    units = []
     for a_y in range(2):
-        groups += [("x", a_y, 0, 0), ("x", a_y, 0, 1)]
-        groups += [("g", a_y, gq) for gq in range(4)]
-    groups += [("x", 0, 1, 0), ("x", 0, 1, 1)]
+        units += [("x", a_y, 0), ("x", a_y, 1)]
+        units += [("g", a_y, gq) for gq in range(4)]
+    units += [("x", 0, 2), ("x", 0, 3), ("x", 1, 2), ("x", 1, 3)]
+    groups = [("xc", 0, 0, [0]), ("xc", 0, 1, [1])]
+    groups += [("g", 0, gq, [2 + gq]) for gq in range(4)]
+    groups += [("xp", 1, 0, 0, [6, 7]), ("xp", 1, 0, 1, [6, 7])]
+    groups += [("g", 1, gq, [8 + gq]) for gq in range(4)]
+    groups += [("xp", 0, 1, 0, [12, 13]), ("xp", 0, 1, 1, [12, 13])]
+    groups += [("xp", 1, 1, 0, [14, 15]), ("xp", 1, 1, 1, [14, 15])]
+    last_reader = {}
+    for i, grp in enumerate(groups):
+        for u in grp[-1]:
+            last_reader[u] = i
 
     with ExitStack() as ctx:
         keep = ctx.enter_context(tc.tile_pool(name="keep", bufs=1))
-        rawp = ctx.enter_context(tc.tile_pool(name="rawp", bufs=3))
+        rawp = ctx.enter_context(tc.tile_pool(name="rawp", bufs=RAW_BUFS))
         grpp = ctx.enter_context(tc.tile_pool(name="grpp", bufs=3))
         outp = ctx.enter_context(tc.tile_pool(name="outp", bufs=8))
         psum = ctx.enter_context(tc.psum_pool(name="psum", bufs=1))
@@ -37,94 +56,85 @@ def tile_patchpositionembedding_kernel(tc, x, W, b, class_token, pos_emb, grad_o
         gc = keep.tile([128, 8192], U32, name="gc", align_bytes=64)
         gs = keep.tile([128, 8192], U8, name="gs", align_bytes=64)
 
-        xtile = {}
-        gtile = {}
+        raw = {}
 
-        def load_x(a_y, h):
-            t = rawp.tile([128, 8192], BF16, name="xraw", tag="xraw", align_bytes=64)
-            xtile[(a_y, h)] = t
-            for r in range(4):
-                for base, b0, nb, a_x in WINDOWS:
-                    gh = 8 * (r // 2) + 4 * a_x + 2 * a_y + (r % 2)
-                    p0 = base + r
-                    nc.sync.dma_start(
-                        out=t[p0 : p0 + 4 * nb - 3 : 4, :].rearrange("p (c f) -> p c f", c=2),
-                        in_=x[b0 : b0 + nb, 2 * h : 2 * h + 2, gh * 16 : gh * 16 + 16, :].rearrange(
-                            "b c h w -> b c (h w)"
-                        ),
-                    )
-
-        def load_g(a_y, pr):
-            t = rawp.tile([128, 8192], BF16, name="graw", tag="graw", align_bytes=64)
-            gtile[(a_y, pr)] = t
-            if G3DIM:
-                for gh0 in range(2):
-                    for base, b0, nb, a_x in WINDOWS:
-                        p0 = base + gh0
-                        off = ((4 * a_x + 2 * a_y + gh0) * 16 + pr * 8) * 1024
-                        nc.sync.dma_start(
-                            out=t[p0 : p0 + 4 * nb - 1 : 2, :].rearrange("(b g) f -> b g f", g=2),
-                            in_=grad_out[b0 : b0 + nb, 1:257, :].rearrange("b (g t) e -> b g (t e)", g=2)[
-                                :, :, off : off + 8192
-                            ],
-                        )
+        def load_piece(u, a_x, r, p0, b0, nb):
+            kind, a_y, sel = units[u]
+            gh = 8 * (r // 2) + 4 * a_x + 2 * a_y + (r % 2)
+            dst = raw[u][p0 : p0 + 4 * nb - 3 : 4, :]
+            if kind == "x":
+                src = x[b0 : b0 + nb, sel : sel + 1, gh * 16 : gh * 16 + 16, :].rearrange("b c h w -> b (c h w)")
             else:
-                for r in range(4):
-                    for base, b0, nb, a_x in WINDOWS:
-                        gh = 8 * (r // 2) + 4 * a_x + 2 * a_y + (r % 2)
-                        t0 = 1 + gh * 16 + pr * 8
-                        p0 = base + r
-                        nc.sync.dma_start(
-                            out=t[p0 : p0 + 4 * nb - 3 : 4, :],
-                            in_=grad_out[b0 : b0 + nb, t0 : t0 + 8, :].rearrange("b t e -> b (t e)"),
-                        )
+                t0 = 1 + gh * 16 + sel * 4
+                src = grad_out[b0 : b0 + nb, t0 : t0 + 4, :].rearrange("b t e -> b (t e)")
+            if p0 >= 96:
+                nc.gpsimd.dma_start(out=dst, in_=src)
+            else:
+                nc.sync.dma_start(out=dst, in_=src)
+
+        def load_unit(u):
+            if u not in raw:
+                raw[u] = rawp.tile([128, 4096], BF16, name="raw", tag="raw", align_bytes=64)
+            for r in range(4):
+                for a_x in range(2):
+                    if SKEW and u == 15 and r == 0 and a_x == 1:
+                        load_piece(u, 1, 0, 96, 8, 8)
+                        continue
+                    for p0, b0, nb in parts(a_x, r):
+                        load_piece(u, a_x, r, p0, b0, nb)
 
         def x_base(a_y, h, gq):
             return ((a_y * 2 + h) * 4 + gq) * 512
 
-        def x_copy(eng_copy, dst_tile, slot, a_y, h, gq):
-            src = xtile[(a_y, h)][:].rearrange("p (cph gq j pw) -> p gq cph pw j", cph=32, gq=4, j=4, pw=16)[:, gq]
-            dst = dst_tile[:, slot * 2048 : slot * 2048 + 2048].rearrange(
-                "p (cph pw j) -> p cph pw j", cph=32, pw=16, j=4
+        grouped = {}
+
+        def x_granule(eng_copy, i, slot, u, gq):
+            src = raw[u][:].rearrange("p (ph gq j pw) -> p gq ph pw j", ph=16, gq=4, j=4, pw=16)[:, gq]
+            dst = grouped[i][:, slot * 1024 : slot * 1024 + 1024].rearrange(
+                "p (ph pw j) -> p ph pw j", ph=16, pw=16, j=4
             )
             eng_copy(out=dst, in_=src)
 
-        def x_quant(src_tile, slot, n, a_y, h, gq):
-            o = x_base(a_y, h, gq)
-            nc.vector.quantize_mx(
-                out=xc[:, o : o + 512 * n].bitcast(E4),
-                scales=xs[:, o : o + 512 * n],
-                in_=src_tile[:, slot * 2048 : (slot + n) * 2048],
-            )
-
-        grouped = {}
-
-        def new_grouped(i):
-            grouped[i] = grpp.tile([128, 4096], BF16, name="grouped", tag="grouped", align_bytes=64)
-            return grouped[i]
-
         def copies(i):
             grp = groups[i]
-            t = new_grouped(i)
+            grouped[i] = grpp.tile([128, 4096], BF16, name="grouped", tag="grouped", align_bytes=64)
             if grp[0] == "g":
-                o = (grp[2] % 2) * 4096
-                src = gtile[(grp[1], grp[2] // 2)][:, o : o + 4096].rearrange("p (j e) -> p e j", j=4)
-                dst = t[:].rearrange("p (e j) -> p e j", j=4)
+                src = raw[grp[3][0]][:].rearrange("p (j e) -> p e j", j=4)
+                dst = grouped[i][:].rearrange("p (e j) -> p e j", j=4)
                 nc.vector.tensor_copy(out=dst[:, 0:512, :], in_=src[:, 0:512, :])
                 nc.scalar.copy(out=dst[:, 512:1024, :], in_=src[:, 512:1024, :])
+            elif grp[0] == "xc":
+                u = grp[3][0]
+                x_granule(nc.vector.tensor_copy, i, 0, u, 0)
+                x_granule(nc.vector.tensor_copy, i, 1, u, 1)
+                x_granule(nc.scalar.copy, i, 2, u, 2)
+                x_granule(nc.scalar.copy, i, 3, u, 3)
             else:
-                x_copy(nc.vector.tensor_copy, t, 0, grp[1], grp[2], 2 * grp[3])
-                x_copy(nc.scalar.copy, t, 1, grp[1], grp[2], 2 * grp[3] + 1)
+                pair = grp[3]
+                u0, u1 = grp[4]
+                x_granule(nc.vector.tensor_copy, i, 0, u0, 2 * pair)
+                x_granule(nc.vector.tensor_copy, i, 1, u1, 2 * pair)
+                x_granule(nc.scalar.copy, i, 2, u0, 2 * pair + 1)
+                x_granule(nc.scalar.copy, i, 3, u1, 2 * pair + 1)
 
         def quantise(i):
             grp = groups[i]
+            t = grouped[i]
             if grp[0] == "g":
                 o = (grp[1] * 4 + grp[2]) * 1024
-                nc.vector.quantize_mx(
-                    out=gc[:, o : o + 1024].bitcast(E5), scales=gs[:, o : o + 1024], in_=grouped[i][:]
-                )
+                nc.vector.quantize_mx(out=gc[:, o : o + 1024].bitcast(E5), scales=gs[:, o : o + 1024], in_=t[:])
+            elif grp[0] == "xc":
+                a_y, c = grp[1], grp[2]
+                for gq in range(4):
+                    o = x_base(a_y, c // 2, gq) + (c % 2) * 256
+                    nc.vector.quantize_mx(
+                        out=xc[:, o : o + 256].bitcast(E4),
+                        scales=xs[:, o : o + 256],
+                        in_=t[:, gq * 1024 : gq * 1024 + 1024],
+                    )
             else:
-                x_quant(grouped[i], 0, 2, grp[1], grp[2], 2 * grp[3])
+                o = x_base(grp[1], grp[2], 2 * grp[3])
+                nc.vector.quantize_mx(out=xc[:, o : o + 1024].bitcast(E4), scales=xs[:, o : o + 1024], in_=t[:])
 
         acc = {}
 
@@ -151,7 +161,7 @@ def tile_patchpositionembedding_kernel(tc, x, W, b, class_token, pos_emb, grad_o
             if grp[0] == "g":
                 for m in range(8):
                     mm(m, 0, grp[1], grp[2])
-            elif grp[2] == 1:
+            elif grp[0] == "xp" and grp[2] == 1:
                 for m in range(8):
                     mm(m, 1, grp[1], 2 * grp[3])
                     mm(m, 1, grp[1], 2 * grp[3] + 1)
@@ -165,23 +175,24 @@ def tile_patchpositionembedding_kernel(tc, x, W, b, class_token, pos_emb, grad_o
         def store(m, h):
             nc.sync.dma_start(out=out[m * 128 : m * 128 + 128, h * 512 : h * 512 + 512], in_=res[m][:])
 
-        load_x(0, 0)
-        load_g(0, 0)
-        load_g(0, 1)
-        load_x(1, 0)
-        load_g(1, 0)
+        if SKEW:
+            raw[15] = keep.tile([128, 4096], BF16, name="raw15", align_bytes=64)
+            load_piece(15, 1, 0, 64, 0, 8)
+        n_rot = 15 if SKEW else 16
+        next_unit = 0
+        while next_unit < RAW_BUFS:
+            load_unit(next_unit)
+            next_unit += 1
         new_banks()
-        n = len(groups)
-        for i in range(n + 1):
+        for i in range(len(groups) + 1):
             if i == 13:
                 for m in (0, 2, 4, 6):
                     evacuate(nc.scalar.copy, m)
-            if i < n:
+            if i < len(groups):
                 copies(i)
-            if i == 3:
-                load_g(1, 1)
-                load_x(0, 1)
-                load_x(1, 1)
+                while next_unit < 16 and (next_unit >= n_rot or last_reader[next_unit - RAW_BUFS] <= i):
+                    load_unit(next_unit)
+                    next_unit += 1
             if i >= 1:
                 quantise(i - 1)
             if i == 13:
@@ -192,22 +203,6 @@ def tile_patchpositionembedding_kernel(tc, x, W, b, class_token, pos_emb, grad_o
                 new_banks()
             if i >= 1:
                 multiply(i - 1)
-        ta = new_grouped(14)
-        tb = new_grouped(15)
-        x_copy(nc.vector.tensor_copy, ta, 0, 1, 1, 0)
-        x_copy(nc.scalar.copy, ta, 1, 1, 1, 1)
-        x_quant(ta, 0, 1, 1, 1, 0)
         for m in range(8):
-            mm(m, 1, 1, 0)
-        x_copy(nc.vector.tensor_copy, tb, 0, 1, 1, 2)
-        x_copy(nc.scalar.copy, tb, 1, 1, 1, 3)
-        x_quant(ta, 1, 1, 1, 1, 1)
-        for m in range(8):
-            mm(m, 1, 1, 1)
-        x_quant(tb, 0, 1, 1, 1, 2)
-        x_quant(tb, 1, 1, 1, 1, 3)
-        for m in range(8):
-            mm(m, 1, 1, 2)
-            mm(m, 1, 1, 3)
             evacuate(nc.scalar.copy if m % 2 == 0 else nc.vector.tensor_copy, m)
             store(m, 1)

@@ -12,42 +12,23 @@ E5 = mybir.dt.float8_e5m2_x4
 FLOPS = 2 * 4096 * 1024 * 1024
 BYTES = 16 * 4 * 256 * 256 * 2 + 16 * 256 * 1024 * 2 + 1024 * 1024 * 4
 
-PLAN = "B"
-SKEW = False
-RAW_BUFS = 8
-
-
-def parts(a_x, r):
-    if PLAN == "W":
-        return [(64 * a_x + r, 0, 16)]
-    if a_x == 0:
-        return [(32 + r, 0, 16)]
-    return [(r, 0, 8), (96 + r, 8, 8)]
+G3DIM = False
+WINDOWS = ((0, 0, 16, 0), (64, 0, 16, 1))
 
 
 def tile_patchpositionembedding_kernel(tc, x, W, b, class_token, pos_emb, grad_out, out):
     nc = tc.nc
-    units = []
+    groups = []
     for a_y in range(2):
-        units += [("x", a_y, 0), ("x", a_y, 1)]
-        units += [("g", a_y, gq) for gq in range(4)]
-    units += [("x", 0, 2), ("x", 0, 3), ("x", 1, 2), ("x", 1, 3)]
-    groups = [("xc", 0, 0, [0]), ("xc", 0, 1, [1])]
-    groups += [("g", 0, gq, [2 + gq]) for gq in range(4)]
-    groups += [("xp", 1, 0, 0, [6, 7]), ("xp", 1, 0, 1, [6, 7])]
-    groups += [("g", 1, gq, [8 + gq]) for gq in range(4)]
-    groups += [("xp", 0, 1, 0, [12, 13]), ("xp", 0, 1, 1, [12, 13])]
-    groups += [("xp", 1, 1, 0, [14, 15]), ("xp", 1, 1, 1, [14, 15])]
-    last_reader = {}
-    for i, grp in enumerate(groups):
-        for u in grp[-1]:
-            last_reader[u] = i
+        groups += [("x", a_y, 0, 0), ("x", a_y, 0, 1)]
+        groups += [("g", a_y, gq) for gq in range(4)]
+    groups += [("x", 0, 1, 0), ("x", 0, 1, 1)]
 
     with ExitStack() as ctx:
         keep = ctx.enter_context(tc.tile_pool(name="keep", bufs=1))
-        rawp = ctx.enter_context(tc.tile_pool(name="rawp", bufs=RAW_BUFS))
+        rawp = ctx.enter_context(tc.tile_pool(name="rawp", bufs=3))
         grpp = ctx.enter_context(tc.tile_pool(name="grpp", bufs=3))
-        outp = ctx.enter_context(tc.tile_pool(name="outp", bufs=8))
+        outp = ctx.enter_context(tc.tile_pool(name="outp", bufs=6))
         psum = ctx.enter_context(tc.psum_pool(name="psum", bufs=1))
         ctx.enter_context(tc.manual_schedule())
 
@@ -56,85 +37,101 @@ def tile_patchpositionembedding_kernel(tc, x, W, b, class_token, pos_emb, grad_o
         gc = keep.tile([128, 8192], U32, name="gc", align_bytes=64)
         gs = keep.tile([128, 8192], U8, name="gs", align_bytes=64)
 
-        raw = {}
+        xtile = {}
+        gtile = {}
 
-        def load_piece(u, a_x, r, p0, b0, nb):
-            kind, a_y, sel = units[u]
+        def x_piece(a_y, h, r, base, b0, nb, a_x):
             gh = 8 * (r // 2) + 4 * a_x + 2 * a_y + (r % 2)
-            dst = raw[u][p0 : p0 + 4 * nb - 3 : 4, :]
-            if kind == "x":
-                src = x[b0 : b0 + nb, sel : sel + 1, gh * 16 : gh * 16 + 16, :].rearrange("b c h w -> b (c h w)")
-            else:
-                t0 = 1 + gh * 16 + sel * 4
-                src = grad_out[b0 : b0 + nb, t0 : t0 + 4, :].rearrange("b t e -> b (t e)")
-            if p0 >= 96:
-                nc.gpsimd.dma_start(out=dst, in_=src)
-            else:
-                nc.sync.dma_start(out=dst, in_=src)
+            p0 = base + r
+            nc.sync.dma_start(
+                out=xtile[(a_y, h)][p0 : p0 + 4 * nb - 3 : 4, :].rearrange("p (c f) -> p c f", c=2),
+                in_=x[b0 : b0 + nb, 2 * h : 2 * h + 2, gh * 16 : gh * 16 + 16, :].rearrange("b c h w -> b c (h w)"),
+            )
 
-        def load_unit(u):
-            if u not in raw:
-                raw[u] = rawp.tile([128, 4096], BF16, name="raw", tag="raw", align_bytes=64)
+        def load_x(a_y, h):
+            if (a_y, h) == (1, 1):
+                x_piece(1, 1, 0, 0, 0, 16, 0)
+                for r in range(1, 4):
+                    x_piece(1, 1, r, 64, 0, 16, 1)
+                    x_piece(1, 1, r, 0, 0, 16, 0)
+                x_piece(1, 1, 0, 96, 8, 8, 1)
+                return
+            xtile[(a_y, h)] = rawp.tile([128, 8192], BF16, name="xraw", tag="xraw", align_bytes=64)
             for r in range(4):
-                for a_x in range(2):
-                    if SKEW and u == 15 and r == 0 and a_x == 1:
-                        load_piece(u, 1, 0, 96, 8, 8)
-                        continue
-                    for p0, b0, nb in parts(a_x, r):
-                        load_piece(u, a_x, r, p0, b0, nb)
+                for base, b0, nb, a_x in WINDOWS:
+                    x_piece(a_y, h, r, base, b0, nb, a_x)
+
+        def load_g(a_y, pr):
+            t = rawp.tile([128, 8192], BF16, name="graw", tag="graw", align_bytes=64)
+            gtile[(a_y, pr)] = t
+            if G3DIM:
+                for gh0 in range(2):
+                    for base, b0, nb, a_x in WINDOWS:
+                        p0 = base + gh0
+                        off = ((4 * a_x + 2 * a_y + gh0) * 16 + pr * 8) * 1024
+                        nc.sync.dma_start(
+                            out=t[p0 : p0 + 4 * nb - 1 : 2, :].rearrange("(b g) f -> b g f", g=2),
+                            in_=grad_out[b0 : b0 + nb, 1:257, :].rearrange("b (g t) e -> b g (t e)", g=2)[
+                                :, :, off : off + 8192
+                            ],
+                        )
+            else:
+                for r in range(4):
+                    for base, b0, nb, a_x in WINDOWS:
+                        gh = 8 * (r // 2) + 4 * a_x + 2 * a_y + (r % 2)
+                        t0 = 1 + gh * 16 + pr * 8
+                        p0 = base + r
+                        nc.sync.dma_start(
+                            out=t[p0 : p0 + 4 * nb - 3 : 4, :],
+                            in_=grad_out[b0 : b0 + nb, t0 : t0 + 8, :].rearrange("b t e -> b (t e)"),
+                        )
 
         def x_base(a_y, h, gq):
             return ((a_y * 2 + h) * 4 + gq) * 512
 
-        grouped = {}
-
-        def x_granule(eng_copy, i, slot, u, gq):
-            src = raw[u][:].rearrange("p (ph gq j pw) -> p gq ph pw j", ph=16, gq=4, j=4, pw=16)[:, gq]
-            dst = grouped[i][:, slot * 1024 : slot * 1024 + 1024].rearrange(
-                "p (ph pw j) -> p ph pw j", ph=16, pw=16, j=4
+        def x_copy(eng_copy, dst_tile, slot, a_y, h, gq):
+            src = xtile[(a_y, h)][:].rearrange("p (cph gq j pw) -> p gq cph pw j", cph=32, gq=4, j=4, pw=16)[:, gq]
+            dst = dst_tile[:, slot * 2048 : slot * 2048 + 2048].rearrange(
+                "p (cph pw j) -> p cph pw j", cph=32, pw=16, j=4
             )
             eng_copy(out=dst, in_=src)
 
+        def x_quant(src_tile, slot, n, a_y, h, gq):
+            o = x_base(a_y, h, gq)
+            nc.vector.quantize_mx(
+                out=xc[:, o : o + 512 * n].bitcast(E4),
+                scales=xs[:, o : o + 512 * n],
+                in_=src_tile[:, slot * 2048 : (slot + n) * 2048],
+            )
+
+        grouped = {}
+
+        def new_grouped(i):
+            grouped[i] = grpp.tile([128, 4096], BF16, name="grouped", tag="grouped", align_bytes=64)
+            return grouped[i]
+
         def copies(i):
             grp = groups[i]
-            grouped[i] = grpp.tile([128, 4096], BF16, name="grouped", tag="grouped", align_bytes=64)
+            t = new_grouped(i)
             if grp[0] == "g":
-                src = raw[grp[3][0]][:].rearrange("p (j e) -> p e j", j=4)
-                dst = grouped[i][:].rearrange("p (e j) -> p e j", j=4)
+                o = (grp[2] % 2) * 4096
+                src = gtile[(grp[1], grp[2] // 2)][:, o : o + 4096].rearrange("p (j e) -> p e j", j=4)
+                dst = t[:].rearrange("p (e j) -> p e j", j=4)
                 nc.vector.tensor_copy(out=dst[:, 0:512, :], in_=src[:, 0:512, :])
                 nc.scalar.copy(out=dst[:, 512:1024, :], in_=src[:, 512:1024, :])
-            elif grp[0] == "xc":
-                u = grp[3][0]
-                x_granule(nc.vector.tensor_copy, i, 0, u, 0)
-                x_granule(nc.vector.tensor_copy, i, 1, u, 1)
-                x_granule(nc.scalar.copy, i, 2, u, 2)
-                x_granule(nc.scalar.copy, i, 3, u, 3)
             else:
-                pair = grp[3]
-                u0, u1 = grp[4]
-                x_granule(nc.vector.tensor_copy, i, 0, u0, 2 * pair)
-                x_granule(nc.vector.tensor_copy, i, 1, u1, 2 * pair)
-                x_granule(nc.scalar.copy, i, 2, u0, 2 * pair + 1)
-                x_granule(nc.scalar.copy, i, 3, u1, 2 * pair + 1)
+                x_copy(nc.vector.tensor_copy, t, 0, grp[1], grp[2], 2 * grp[3])
+                x_copy(nc.scalar.copy, t, 1, grp[1], grp[2], 2 * grp[3] + 1)
 
         def quantise(i):
             grp = groups[i]
-            t = grouped[i]
             if grp[0] == "g":
                 o = (grp[1] * 4 + grp[2]) * 1024
-                nc.vector.quantize_mx(out=gc[:, o : o + 1024].bitcast(E5), scales=gs[:, o : o + 1024], in_=t[:])
-            elif grp[0] == "xc":
-                a_y, c = grp[1], grp[2]
-                for gq in range(4):
-                    o = x_base(a_y, c // 2, gq) + (c % 2) * 256
-                    nc.vector.quantize_mx(
-                        out=xc[:, o : o + 256].bitcast(E4),
-                        scales=xs[:, o : o + 256],
-                        in_=t[:, gq * 1024 : gq * 1024 + 1024],
-                    )
+                nc.vector.quantize_mx(
+                    out=gc[:, o : o + 1024].bitcast(E5), scales=gs[:, o : o + 1024], in_=grouped[i][:]
+                )
             else:
-                o = x_base(grp[1], grp[2], 2 * grp[3])
-                nc.vector.quantize_mx(out=xc[:, o : o + 1024].bitcast(E4), scales=xs[:, o : o + 1024], in_=t[:])
+                x_quant(grouped[i], 0, 2, grp[1], grp[2], 2 * grp[3])
 
         acc = {}
 
@@ -161,7 +158,7 @@ def tile_patchpositionembedding_kernel(tc, x, W, b, class_token, pos_emb, grad_o
             if grp[0] == "g":
                 for m in range(8):
                     mm(m, 0, grp[1], grp[2])
-            elif grp[0] == "xp" and grp[2] == 1:
+            elif grp[2] == 1:
                 for m in range(8):
                     mm(m, 1, grp[1], 2 * grp[3])
                     mm(m, 1, grp[1], 2 * grp[3] + 1)
@@ -175,24 +172,25 @@ def tile_patchpositionembedding_kernel(tc, x, W, b, class_token, pos_emb, grad_o
         def store(m, h):
             nc.sync.dma_start(out=out[m * 128 : m * 128 + 128, h * 512 : h * 512 + 512], in_=res[m][:])
 
-        if SKEW:
-            raw[15] = keep.tile([128, 4096], BF16, name="raw15", align_bytes=64)
-            load_piece(15, 1, 0, 64, 0, 8)
-        n_rot = 15 if SKEW else 16
-        next_unit = 0
-        while next_unit < RAW_BUFS:
-            load_unit(next_unit)
-            next_unit += 1
+        xtile[(1, 1)] = keep.tile([128, 8192], BF16, name="xlast", align_bytes=64)
+        x_piece(1, 1, 0, 64, 0, 8, 1)
+        load_x(0, 0)
+        load_g(0, 0)
+        load_g(0, 1)
+        load_x(1, 0)
+        load_g(1, 0)
         new_banks()
-        for i in range(len(groups) + 1):
+        n = len(groups)
+        for i in range(n + 1):
             if i == 13:
                 for m in (0, 2, 4, 6):
                     evacuate(nc.scalar.copy, m)
-            if i < len(groups):
+            if i < n:
                 copies(i)
-                while next_unit < 16 and (next_unit >= n_rot or last_reader[next_unit - RAW_BUFS] <= i):
-                    load_unit(next_unit)
-                    next_unit += 1
+            if i == 3:
+                load_g(1, 1)
+                load_x(0, 1)
+                load_x(1, 1)
             if i >= 1:
                 quantise(i - 1)
             if i == 13:
@@ -203,6 +201,22 @@ def tile_patchpositionembedding_kernel(tc, x, W, b, class_token, pos_emb, grad_o
                 new_banks()
             if i >= 1:
                 multiply(i - 1)
+        ta = new_grouped(14)
+        tb = new_grouped(15)
+        x_copy(nc.vector.tensor_copy, ta, 0, 1, 1, 0)
+        x_copy(nc.scalar.copy, ta, 1, 1, 1, 1)
+        x_quant(ta, 0, 1, 1, 1, 0)
         for m in range(8):
+            mm(m, 1, 1, 0)
+        x_copy(nc.vector.tensor_copy, tb, 0, 1, 1, 2)
+        x_copy(nc.scalar.copy, tb, 1, 1, 1, 3)
+        x_quant(ta, 1, 1, 1, 1, 1)
+        for m in range(8):
+            mm(m, 1, 1, 1)
+        x_quant(tb, 0, 1, 1, 1, 2)
+        x_quant(tb, 1, 1, 1, 1, 3)
+        for m in range(8):
+            mm(m, 1, 1, 2)
+            mm(m, 1, 1, 3)
             evacuate(nc.scalar.copy if m % 2 == 0 else nc.vector.tensor_copy, m)
             store(m, 1)

@@ -12,23 +12,24 @@ E5 = mybir.dt.float8_e5m2_x4
 FLOPS = 2 * 4096 * 1024 * 1024
 BYTES = 16 * 4 * 256 * 256 * 2 + 16 * 256 * 1024 * 2 + 1024 * 1024 * 4
 
-G3DIM = False
-WINDOWS = ((0, 0, 16, 0), (64, 0, 16, 1))
+RAW_BUFS = 8
+WINDOWS = ((32, 0, 16, 0), (0, 0, 8, 1), (96, 8, 8, 1))
+G_SPLIT = 672
 
 
 def tile_patchpositionembedding_kernel(tc, x, W, b, class_token, pos_emb, grad_out, out):
     nc = tc.nc
-    groups = []
+    units = []
     for a_y in range(2):
-        groups += [("x", a_y, 0, 0), ("x", a_y, 0, 1)]
-        groups += [("g", a_y, gq) for gq in range(4)]
-    groups += [("x", 0, 1, 0), ("x", 0, 1, 1)]
+        units += [("x", a_y, 0), ("x", a_y, 1)]
+        units += [("g", a_y, gq) for gq in range(4)]
+    units += [("x", 0, 2), ("x", 0, 3), ("x", 1, 2), ("x", 1, 3)]
 
     with ExitStack() as ctx:
         keep = ctx.enter_context(tc.tile_pool(name="keep", bufs=1))
-        rawp = ctx.enter_context(tc.tile_pool(name="rawp", bufs=3))
-        grpp = ctx.enter_context(tc.tile_pool(name="grpp", bufs=3))
-        outp = ctx.enter_context(tc.tile_pool(name="outp", bufs=6))
+        rawp = ctx.enter_context(tc.tile_pool(name="rawp", bufs=RAW_BUFS))
+        grpp = ctx.enter_context(tc.tile_pool(name="grpp", bufs=4))
+        outp = ctx.enter_context(tc.tile_pool(name="outp", bufs=8))
         psum = ctx.enter_context(tc.psum_pool(name="psum", bufs=1))
         ctx.enter_context(tc.manual_schedule())
 
@@ -37,101 +38,47 @@ def tile_patchpositionembedding_kernel(tc, x, W, b, class_token, pos_emb, grad_o
         gc = keep.tile([128, 8192], U32, name="gc", align_bytes=64)
         gs = keep.tile([128, 8192], U8, name="gs", align_bytes=64)
 
-        xtile = {}
-        gtile = {}
+        raw = {}
 
-        def x_piece(a_y, h, r, base, b0, nb, a_x):
-            gh = 8 * (r // 2) + 4 * a_x + 2 * a_y + (r % 2)
-            p0 = base + r
-            nc.sync.dma_start(
-                out=xtile[(a_y, h)][p0 : p0 + 4 * nb - 3 : 4, :].rearrange("p (c f) -> p c f", c=2),
-                in_=x[b0 : b0 + nb, 2 * h : 2 * h + 2, gh * 16 : gh * 16 + 16, :].rearrange("b c h w -> b c (h w)"),
-            )
-
-        def load_x(a_y, h):
-            if (a_y, h) == (1, 1):
-                x_piece(1, 1, 0, 0, 0, 16, 0)
-                for r in range(1, 4):
-                    x_piece(1, 1, r, 64, 0, 16, 1)
-                    x_piece(1, 1, r, 0, 0, 16, 0)
-                x_piece(1, 1, 0, 96, 8, 8, 1)
-                return
-            xtile[(a_y, h)] = rawp.tile([128, 8192], BF16, name="xraw", tag="xraw", align_bytes=64)
+        def load_unit(u):
+            kind, a_y, sel = units[u]
+            raw[u] = rawp.tile([128, 4096], BF16, name="raw", tag="raw", align_bytes=64)
             for r in range(4):
                 for base, b0, nb, a_x in WINDOWS:
-                    x_piece(a_y, h, r, base, b0, nb, a_x)
-
-        def load_g(a_y, pr):
-            t = rawp.tile([128, 8192], BF16, name="graw", tag="graw", align_bytes=64)
-            gtile[(a_y, pr)] = t
-            if G3DIM:
-                for gh0 in range(2):
-                    for base, b0, nb, a_x in WINDOWS:
-                        p0 = base + gh0
-                        off = ((4 * a_x + 2 * a_y + gh0) * 16 + pr * 8) * 1024
-                        nc.sync.dma_start(
-                            out=t[p0 : p0 + 4 * nb - 1 : 2, :].rearrange("(b g) f -> b g f", g=2),
-                            in_=grad_out[b0 : b0 + nb, 1:257, :].rearrange("b (g t) e -> b g (t e)", g=2)[
-                                :, :, off : off + 8192
-                            ],
+                    gh = 8 * (r // 2) + 4 * a_x + 2 * a_y + (r % 2)
+                    p0 = base + r
+                    if kind == "x":
+                        src = x[b0 : b0 + nb, sel : sel + 1, gh * 16 : gh * 16 + 16, :].rearrange(
+                            "b c h w -> b (c h w)"
                         )
-            else:
-                for r in range(4):
-                    for base, b0, nb, a_x in WINDOWS:
-                        gh = 8 * (r // 2) + 4 * a_x + 2 * a_y + (r % 2)
-                        t0 = 1 + gh * 16 + pr * 8
-                        p0 = base + r
-                        nc.sync.dma_start(
-                            out=t[p0 : p0 + 4 * nb - 3 : 4, :],
-                            in_=grad_out[b0 : b0 + nb, t0 : t0 + 8, :].rearrange("b t e -> b (t e)"),
-                        )
+                    else:
+                        t0 = 1 + gh * 16 + sel * 4
+                        src = grad_out[b0 : b0 + nb, t0 : t0 + 4, :].rearrange("b t e -> b (t e)")
+                    nc.sync.dma_start(out=raw[u][p0 : p0 + 4 * nb - 3 : 4, :], in_=src)
 
         def x_base(a_y, h, gq):
             return ((a_y * 2 + h) * 4 + gq) * 512
 
-        def x_copy(eng_copy, dst_tile, slot, a_y, h, gq):
-            src = xtile[(a_y, h)][:].rearrange("p (cph gq j pw) -> p gq cph pw j", cph=32, gq=4, j=4, pw=16)[:, gq]
-            dst = dst_tile[:, slot * 2048 : slot * 2048 + 2048].rearrange(
-                "p (cph pw j) -> p cph pw j", cph=32, pw=16, j=4
-            )
+        def new_grouped():
+            return grpp.tile([128, 4096], BF16, name="grouped", tag="grouped", align_bytes=64)
+
+        pair = {}
+
+        def x_copy(eng_copy, u, gq):
+            c = units[u][2]
+            src = raw[u][:].rearrange("p (ph gq j pw) -> p gq ph pw j", ph=16, gq=4, j=4, pw=16)[:, gq]
+            o = (gq % 2) * 2048 + (c % 2) * 1024
+            dst = pair[gq // 2][:, o : o + 1024].rearrange("p (ph pw j) -> p ph pw j", ph=16, pw=16, j=4)
             eng_copy(out=dst, in_=src)
 
-        def x_quant(src_tile, slot, n, a_y, h, gq):
+        def x_quant(a_y, h, gq, n):
             o = x_base(a_y, h, gq)
+            s = (gq % 2) * 2048
             nc.vector.quantize_mx(
                 out=xc[:, o : o + 512 * n].bitcast(E4),
                 scales=xs[:, o : o + 512 * n],
-                in_=src_tile[:, slot * 2048 : (slot + n) * 2048],
+                in_=pair[gq // 2][:, s : s + 2048 * n],
             )
-
-        grouped = {}
-
-        def new_grouped(i):
-            grouped[i] = grpp.tile([128, 4096], BF16, name="grouped", tag="grouped", align_bytes=64)
-            return grouped[i]
-
-        def copies(i):
-            grp = groups[i]
-            t = new_grouped(i)
-            if grp[0] == "g":
-                o = (grp[2] % 2) * 4096
-                src = gtile[(grp[1], grp[2] // 2)][:, o : o + 4096].rearrange("p (j e) -> p e j", j=4)
-                dst = t[:].rearrange("p (e j) -> p e j", j=4)
-                nc.vector.tensor_copy(out=dst[:, 0:512, :], in_=src[:, 0:512, :])
-                nc.scalar.copy(out=dst[:, 512:1024, :], in_=src[:, 512:1024, :])
-            else:
-                x_copy(nc.vector.tensor_copy, t, 0, grp[1], grp[2], 2 * grp[3])
-                x_copy(nc.scalar.copy, t, 1, grp[1], grp[2], 2 * grp[3] + 1)
-
-        def quantise(i):
-            grp = groups[i]
-            if grp[0] == "g":
-                o = (grp[1] * 4 + grp[2]) * 1024
-                nc.vector.quantize_mx(
-                    out=gc[:, o : o + 1024].bitcast(E5), scales=gs[:, o : o + 1024], in_=grouped[i][:]
-                )
-            else:
-                x_quant(grouped[i], 0, 2, grp[1], grp[2], 2 * grp[3])
 
         acc = {}
 
@@ -153,16 +100,6 @@ def tile_patchpositionembedding_kernel(tc, x, W, b, class_token, pos_emb, grad_o
                 stop=(k == 7),
             )
 
-        def multiply(i):
-            grp = groups[i]
-            if grp[0] == "g":
-                for m in range(8):
-                    mm(m, 0, grp[1], grp[2])
-            elif grp[2] == 1:
-                for m in range(8):
-                    mm(m, 1, grp[1], 2 * grp[3])
-                    mm(m, 1, grp[1], 2 * grp[3] + 1)
-
         res = {}
 
         def evacuate(eng_copy, m):
@@ -172,51 +109,71 @@ def tile_patchpositionembedding_kernel(tc, x, W, b, class_token, pos_emb, grad_o
         def store(m, h):
             nc.sync.dma_start(out=out[m * 128 : m * 128 + 128, h * 512 : h * 512 + 512], in_=res[m][:])
 
-        xtile[(1, 1)] = keep.tile([128, 8192], BF16, name="xlast", align_bytes=64)
-        x_piece(1, 1, 0, 64, 0, 8, 1)
-        load_x(0, 0)
-        load_g(0, 0)
-        load_g(0, 1)
-        load_x(1, 0)
-        load_g(1, 0)
+        def do_g(u):
+            a_y, gq = units[u][1], units[u][2]
+            t = new_grouped()
+            src = raw[u][:].rearrange("p (j e) -> p e j", j=4)
+            dst = t[:].rearrange("p (e j) -> p e j", j=4)
+            nc.vector.tensor_copy(out=dst[:, 0:G_SPLIT, :], in_=src[:, 0:G_SPLIT, :])
+            nc.scalar.copy(out=dst[:, G_SPLIT:1024, :], in_=src[:, G_SPLIT:1024, :])
+            o = (a_y * 4 + gq) * 1024
+            nc.vector.quantize_mx(out=gc[:, o : o + 1024].bitcast(E5), scales=gs[:, o : o + 1024], in_=t[:])
+            for m in range(8):
+                mm(m, 0, a_y, gq)
+
+        def do_x(u):
+            a_y, c = units[u][1], units[u][2]
+            h = c // 2
+            if c % 2 == 0:
+                pair[0] = new_grouped()
+                pair[1] = new_grouped()
+                x_copy(nc.vector.tensor_copy, u, 0)
+                x_copy(nc.vector.tensor_copy, u, 2)
+                x_copy(nc.scalar.copy, u, 1)
+                x_copy(nc.scalar.copy, u, 3)
+                return
+            x_copy(nc.scalar.copy, u, 1)
+            x_copy(nc.scalar.copy, u, 3)
+            if h == 0:
+                x_copy(nc.vector.tensor_copy, u, 0)
+                x_copy(nc.vector.tensor_copy, u, 2)
+                x_quant(a_y, 0, 0, 2)
+                x_quant(a_y, 0, 2, 2)
+                return
+            x_copy(nc.vector.tensor_copy, u, 0)
+            x_quant(a_y, 1, 0, 1)
+            for m in range(8):
+                mm(m, 1, a_y, 0)
+            x_copy(nc.vector.tensor_copy, u, 2)
+            x_quant(a_y, 1, 1, 1)
+            for m in range(8):
+                mm(m, 1, a_y, 1)
+            x_quant(a_y, 1, 2, 1)
+            x_quant(a_y, 1, 3, 1)
+            if a_y == 0:
+                for gq in (2, 3):
+                    for m in range(8):
+                        mm(m, 1, 0, gq)
+            else:
+                for m in range(8):
+                    mm(m, 1, 1, 2)
+                    mm(m, 1, 1, 3)
+                    evacuate(nc.scalar.copy if m % 2 == 0 else nc.vector.tensor_copy, m)
+                    store(m, 1)
+
+        for u in range(RAW_BUFS):
+            load_unit(u)
         new_banks()
-        n = len(groups)
-        for i in range(n + 1):
-            if i == 13:
-                for m in (0, 2, 4, 6):
-                    evacuate(nc.scalar.copy, m)
-            if i < n:
-                copies(i)
-            if i == 3:
-                load_g(1, 1)
-                load_x(0, 1)
-                load_x(1, 1)
-            if i >= 1:
-                quantise(i - 1)
-            if i == 13:
-                for m in (1, 3, 5, 7):
-                    evacuate(nc.vector.tensor_copy, m)
+        for u in range(16):
+            if units[u][0] == "g":
+                do_g(u)
+            else:
+                do_x(u)
+            if u + RAW_BUFS < 16:
+                load_unit(u + RAW_BUFS)
+            if u == 11:
+                for m in range(8):
+                    evacuate(nc.scalar.copy if m % 2 == 0 else nc.vector.tensor_copy, m)
                 for m in range(8):
                     store(m, 0)
                 new_banks()
-            if i >= 1:
-                multiply(i - 1)
-        ta = new_grouped(14)
-        tb = new_grouped(15)
-        x_copy(nc.vector.tensor_copy, ta, 0, 1, 1, 0)
-        x_copy(nc.scalar.copy, ta, 1, 1, 1, 1)
-        x_quant(ta, 0, 1, 1, 1, 0)
-        for m in range(8):
-            mm(m, 1, 1, 0)
-        x_copy(nc.vector.tensor_copy, tb, 0, 1, 1, 2)
-        x_copy(nc.scalar.copy, tb, 1, 1, 1, 3)
-        x_quant(ta, 1, 1, 1, 1, 1)
-        for m in range(8):
-            mm(m, 1, 1, 1)
-        x_quant(tb, 0, 1, 1, 1, 2)
-        x_quant(tb, 1, 1, 1, 1, 3)
-        for m in range(8):
-            mm(m, 1, 1, 2)
-            mm(m, 1, 1, 3)
-            evacuate(nc.scalar.copy if m % 2 == 0 else nc.vector.tensor_copy, m)
-            store(m, 1)

@@ -13,7 +13,7 @@ FLOPS = 2 * 4096 * 1024 * 1024
 BYTES = 16 * 4 * 256 * 256 * 2 + 16 * 256 * 1024 * 2 + 1024 * 1024 * 4
 
 RAW_BUFS = 8
-WINDOWS = ((32, 0, 16, 0), (0, 0, 8, 1), (96, 8, 8, 1))
+WINDOWS = ((32, 0, 16, 0), (96, 8, 8, 1), (0, 0, 8, 1))
 G_SPLIT = 672
 
 
@@ -43,8 +43,8 @@ def tile_patchpositionembedding_kernel(tc, x, W, b, class_token, pos_emb, grad_o
         def load_unit(u):
             kind, a_y, sel = units[u]
             raw[u] = rawp.tile([128, 4096], BF16, name="raw", tag="raw", align_bytes=64)
-            for r in range(4):
-                for base, b0, nb, a_x in WINDOWS:
+            for base, b0, nb, a_x in WINDOWS:
+                for r in range(4):
                     gh = 8 * (r // 2) + 4 * a_x + 2 * a_y + (r % 2)
                     p0 = base + r
                     if kind == "x":

from contextlib import ExitStack

import concourse.mybir as mybir

BF16 = mybir.dt.bfloat16
F32 = mybir.dt.float32
U32 = mybir.dt.uint32
U8 = mybir.dt.uint8
E4 = mybir.dt.float8_e4m3fn_x4
E5 = mybir.dt.float8_e5m2_x4

FLOPS = 2 * 4096 * 1024 * 1024
BYTES = 16 * 4 * 256 * 256 * 2 + 16 * 256 * 1024 * 2 + 1024 * 1024 * 4

RAW_BUFS = 8
WINDOWS = ((32, 0, 16, 0), (96, 8, 8, 1), (0, 0, 8, 1))
G_SPLIT = 672


def tile_patchpositionembedding_kernel(tc, x, W, b, class_token, pos_emb, grad_out, out):
    nc = tc.nc
    units = []
    for a_y in range(2):
        units += [("x", a_y, 0), ("x", a_y, 1)]
        units += [("g", a_y, gq) for gq in range(4)]
    units += [("x", 0, 2), ("x", 0, 3), ("x", 1, 2), ("x", 1, 3)]

    with ExitStack() as ctx:
        keep = ctx.enter_context(tc.tile_pool(name="keep", bufs=1))
        rawp = ctx.enter_context(tc.tile_pool(name="rawp", bufs=RAW_BUFS))
        grpp = ctx.enter_context(tc.tile_pool(name="grpp", bufs=4))
        outp = ctx.enter_context(tc.tile_pool(name="outp", bufs=8))
        psum = ctx.enter_context(tc.psum_pool(name="psum", bufs=1))
        ctx.enter_context(tc.manual_schedule())

        xc = keep.tile([128, 8192], U32, name="xc", align_bytes=64)
        xs = keep.tile([128, 8192], U8, name="xs", align_bytes=64)
        gc = keep.tile([128, 8192], U32, name="gc", align_bytes=64)
        gs = keep.tile([128, 8192], U8, name="gs", align_bytes=64)

        raw = {}

        def load_unit(u):
            kind, a_y, sel = units[u]
            raw[u] = rawp.tile([128, 4096], BF16, name="raw", tag="raw", align_bytes=64)
            for base, b0, nb, a_x in WINDOWS:
                for r in range(4):
                    gh = 8 * (r // 2) + 4 * a_x + 2 * a_y + (r % 2)
                    p0 = base + r
                    if kind == "x":
                        src = x[b0 : b0 + nb, sel : sel + 1, gh * 16 : gh * 16 + 16, :].rearrange(
                            "b c h w -> b (c h w)"
                        )
                    else:
                        t0 = 1 + gh * 16 + sel * 4
                        src = grad_out[b0 : b0 + nb, t0 : t0 + 4, :].rearrange("b t e -> b (t e)")
                    nc.sync.dma_start(out=raw[u][p0 : p0 + 4 * nb - 3 : 4, :], in_=src)

        def x_base(a_y, h, gq):
            return ((a_y * 2 + h) * 4 + gq) * 512

        def new_grouped():
            return grpp.tile([128, 4096], BF16, name="grouped", tag="grouped", align_bytes=64)

        pair = {}

        def x_copy(eng_copy, u, gq):
            c = units[u][2]
            src = raw[u][:].rearrange("p (ph gq j pw) -> p gq ph pw j", ph=16, gq=4, j=4, pw=16)[:, gq]
            o = (gq % 2) * 2048 + (c % 2) * 1024
            dst = pair[gq // 2][:, o : o + 1024].rearrange("p (ph pw j) -> p ph pw j", ph=16, pw=16, j=4)
            eng_copy(out=dst, in_=src)

        def x_quant(a_y, h, gq, n):
            o = x_base(a_y, h, gq)
            s = (gq % 2) * 2048
            nc.vector.quantize_mx(
                out=xc[:, o : o + 512 * n].bitcast(E4),
                scales=xs[:, o : o + 512 * n],
                in_=pair[gq // 2][:, s : s + 2048 * n],
            )

        acc = {}

        def new_banks():
            for m in range(8):
                acc[m] = psum.tile([128, 512], F32, name="acc%d" % m)

        def mm(m, h, a_y, gq):
            k = a_y * 4 + gq
            go = k * 1024 + m * 128
            xo = x_base(a_y, h, gq)
            nc.tensor.matmul_mx(
                out=acc[m][:],
                lhsT=gc[:, go : go + 128].bitcast(E5),
                lhsT_scale=gs[:, go : go + 128],
                rhs=xc[:, xo : xo + 512].bitcast(E4),
                rhs_scale=xs[:, xo : xo + 512],
                start=(k == 0),
                stop=(k == 7),
            )

        res = {}

        def evacuate(eng_copy, m):
            res[m] = outp.tile([128, 512], F32, name="res", tag="res")
            eng_copy(out=res[m][:], in_=acc[m][:])

        def store(m, h):
            nc.sync.dma_start(out=out[m * 128 : m * 128 + 128, h * 512 : h * 512 + 512], in_=res[m][:])

        def do_g(u):
            a_y, gq = units[u][1], units[u][2]
            t = new_grouped()
            src = raw[u][:].rearrange("p (j e) -> p e j", j=4)
            dst = t[:].rearrange("p (e j) -> p e j", j=4)
            nc.vector.tensor_copy(out=dst[:, 0:G_SPLIT, :], in_=src[:, 0:G_SPLIT, :])
            nc.scalar.copy(out=dst[:, G_SPLIT:1024, :], in_=src[:, G_SPLIT:1024, :])
            o = (a_y * 4 + gq) * 1024
            nc.vector.quantize_mx(out=gc[:, o : o + 1024].bitcast(E5), scales=gs[:, o : o + 1024], in_=t[:])
            for m in range(8):
                mm(m, 0, a_y, gq)

        def do_x(u):
            a_y, c = units[u][1], units[u][2]
            h = c // 2
            if c % 2 == 0:
                pair[0] = new_grouped()
                pair[1] = new_grouped()
                x_copy(nc.vector.tensor_copy, u, 0)
                x_copy(nc.vector.tensor_copy, u, 2)
                x_copy(nc.scalar.copy, u, 1)
                x_copy(nc.scalar.copy, u, 3)
                return
            x_copy(nc.scalar.copy, u, 1)
            x_copy(nc.scalar.copy, u, 3)
            if h == 0:
                x_copy(nc.vector.tensor_copy, u, 0)
                x_copy(nc.vector.tensor_copy, u, 2)
                x_quant(a_y, 0, 0, 2)
                x_quant(a_y, 0, 2, 2)
                return
            x_copy(nc.vector.tensor_copy, u, 0)
            x_quant(a_y, 1, 0, 1)
            for m in range(8):
                mm(m, 1, a_y, 0)
            x_copy(nc.vector.tensor_copy, u, 2)
            x_quant(a_y, 1, 1, 1)
            for m in range(8):
                mm(m, 1, a_y, 1)
            x_quant(a_y, 1, 2, 1)
            x_quant(a_y, 1, 3, 1)
            if a_y == 0:
                for gq in (2, 3):
                    for m in range(8):
                        mm(m, 1, 0, gq)
            else:
                for m in range(8):
                    mm(m, 1, 1, 2)
                    mm(m, 1, 1, 3)
                    evacuate(nc.scalar.copy if m % 2 == 0 else nc.vector.tensor_copy, m)
                    store(m, 1)

        for u in range(RAW_BUFS):
            load_unit(u)
        new_banks()
        for u in range(16):
            if units[u][0] == "g":
                do_g(u)
            else:
                do_x(u)
            if u + RAW_BUFS < 16:
                load_unit(u + RAW_BUFS)
            if u == 11:
                for m in range(8):
                    evacuate(nc.scalar.copy if m % 2 == 0 else nc.vector.tensor_copy, m)
                for m in range(8):
                    store(m, 0)
                new_banks()
